import numpy as np
import ml_dtypes


def mxq(x, axis, fmt="e4m3"):
    dtype, down = {"e4m3": (ml_dtypes.float8_e4m3fn, 7), "e5m2": (ml_dtypes.float8_e5m2, 14)}[fmt]
    v = np.moveaxis(np.asarray(x, np.float32).astype(ml_dtypes.bfloat16).astype(np.float64), axis, -1)
    blocks = v.reshape(v.shape[:-1] + (-1, 32))
    amax = np.abs(blocks).max(-1, keepdims=True)
    byte = np.maximum(np.where(amax > 0, np.frexp(amax)[1] - 1 + 127, 0) - down, 1)
    scale = np.exp2(byte - 127.0)
    codes = (blocks / scale).astype(np.float32).astype(dtype).astype(np.float64)
    return np.moveaxis((codes * scale).reshape(v.shape), -1, axis)


WIDE = False


def mx_kscale(k):
    if not WIDE:
        return np.ones(k)
    levels = np.array([30, -30])
    if k % 512:
        return np.exp2(np.random.permutation(np.resize(levels, k // 32))).repeat(32)
    a = np.empty((k // 512, 16))
    for p in range(k // 512):
        a[p, :8] = np.random.permutation(np.resize(levels, 8))
        for g in range(8):
            far = levels[np.abs(levels - a[p, g]) >= 10]
            a[p, g + 8] = far[np.random.randint(len(far))]
    return np.exp2(a.ravel()).repeat(32)


BF16 = ml_dtypes.bfloat16


def bf(x):
    return np.asarray(x, np.float32).astype(BF16)


def f64(x):
    return np.asarray(x).astype(np.float64)


B, N, D, L = 1, 1024, 512, 512
SEGS = N // L


def setup_inputs():
    s = mx_kscale(D)
    col = np.concatenate([np.full(D, np.sqrt(SEGS)), np.ones(D)])
    return {"x": bf(np.random.standard_normal((B, N, D)) * s),
            "w_kv": bf(np.random.standard_normal((D, D + D)) * col / np.sqrt(D) / s[:, None])}


def reference(x, w_kv):
    kv = mxq(f64(x), 2, "e5m2") @ mxq(f64(w_kv), 0, "e5m2")
    k, v = kv[..., :D], kv[..., D:]
    keys_lm = k.reshape(B, L, SEGS, D).mean(axis=2)
    vals_lm = v.reshape(B, L, SEGS, D).mean(axis=2)
    return v, keys_lm, vals_lm

@@ -1,0 +1,198 @@
+from contextlib import ExitStack
+
+import concourse.mybir as mybir
+from concourse.masks import make_identity
+
+TOKENS, K, D = 1024, 512, 512
+FLOPS = 2 * TOKENS * K * (2 * D)
+
+F32 = mybir.dt.float32
+BF16 = mybir.dt.bfloat16
+U32 = mybir.dt.uint32
+U8 = mybir.dt.uint8
+E5X4 = mybir.dt.float8_e5m2_x4
+COPY = mybir.ActivationFunctionType.Copy
+MULT = mybir.AluOpType.mult
+
+P = 128
+PACK = 4
+GROUPS = 4
+W_PART = 256
+V_SHARE = 176
+
+
+def tile_ammattention_pa_kernel(tc, x, w_kv, out_0, out_1, out_2):
+    nc = tc.nc
+
+    x_view = x.flatten_outer_dims().rearrange("(l m e) k -> m l e k", m=P, e=2)
+    w_view = w_kv.rearrange("(p j) n -> p j n", j=PACK)
+    v_view = out_0.flatten_outer_dims().rearrange("(l m e) d -> m l e d", m=P, e=2)
+    klm_view = out_1.flatten_outer_dims().rearrange("(l m) d -> m l d", m=P)
+    vlm_view = out_2.flatten_outer_dims().rearrange("(l m) d -> m l d", m=P)
+
+    with ExitStack() as ctx:
+        keep = ctx.enter_context(tc.tile_pool(name="keep", bufs=1))
+        psum = ctx.enter_context(tc.psum_pool(name="psum", bufs=8))
+        ctx.enter_context(tc.manual_schedule())
+
+        units = [(0, 0, 1), (0, 1, 1), (1, 0, 2), (2, 0, 2), (3, 0, 2)]
+        x_sb = {}
+        w_raw = {}
+        w_grouped = {}
+        w_codes = {}
+        w_scales = {}
+        xt_of = {}
+        x_grouped = {}
+        x_codes = {}
+        x_scales = {}
+
+        def load_x(unit):
+            g, e0, n = unit
+            t = keep.tile([P, n, K], BF16, name="x_sb%d%d" % (g, e0))
+            nc.sync.dma_start(out=t[:], in_=x_view[:, g, e0:e0 + n, :])
+            x_sb[unit] = t
+
+        def load_w(half, part):
+            c0 = (D if half == "v" else 0) + W_PART * part
+            t = keep.tile([P, PACK, W_PART], BF16, name="w_raw_%s%d" % (half, part))
+            nc.sync.dma_start(out=t[:], in_=w_view[:, :, c0:c0 + W_PART])
+            w_raw[(half, part)] = t
+
+        def interleave_w(half, part):
+            src = w_raw[(half, part)]
+            t = keep.tile([P, W_PART, PACK], BF16, name="w_grouped_%s%d" % (half, part), align_bytes=64)
+            nc.vector.tensor_copy(out=t[:, 0:V_SHARE, :], in_=src[:, :, 0:V_SHARE].rearrange("p j c -> p c j"))
+            nc.scalar.copy(out=t[:, V_SHARE:W_PART, :], in_=src[:, :, V_SHARE:W_PART].rearrange("p j c -> p c j"))
+            w_grouped[(half, part)] = t
+
+        def quantize_w(half, part):
+            if part == 0:
+                codes = keep.tile([P, D], U32, name="w_codes_%s" % half, align_bytes=64)
+                scales = keep.tile([P, D], U8, name="w_scales_%s" % half, align_bytes=64)
+                w_codes[half] = codes
+                w_scales[half] = scales
+            cols = slice(W_PART * part, W_PART * (part + 1))
+            nc.vector.quantize_mx(
+                out=w_codes[half][:, cols].bitcast(E5X4),
+                scales=w_scales[half][:, cols],
+                in_=w_grouped[(half, part)][:].rearrange("p c j -> p (c j)"),
+            )
+
+        def transpose_x(unit):
+            g, e0, n = unit
+            xt = psum.tile([P, n, 2, P], F32, name="bank")
+            for i in range(n):
+                words = x_sb[unit][:, i, :].bitcast(F32)
+                for u in range(2):
+                    nc.tensor.transpose(xt[:, i, u, :], words[:, u:K // 2:2], ident[:])
+            xt_of[unit] = xt
+
+        def copy_x(unit):
+            g, e0, n = unit
+            t = keep.tile([P, n, P, PACK], BF16, name="x_grouped%d%d" % (g, e0), align_bytes=64)
+            nc.scalar.copy(out=t[:].bitcast(F32), in_=xt_of[unit][:].rearrange("p e u m -> p e m u"))
+            x_grouped[unit] = t
+
+        def quantize_x(unit):
+            g, e0, n = unit
+            codes = keep.tile([P, n * P], U32, name="x_codes%d%d" % (g, e0), align_bytes=64)
+            scales = keep.tile([P, n * P], U8, name="x_scales%d%d" % (g, e0), align_bytes=64)
+            nc.vector.quantize_mx(
+                out=codes[:].bitcast(E5X4),
+                scales=scales[:],
+                in_=x_grouped[unit][:].rearrange("p e m t -> p (e m t)"),
+            )
+            for i in range(n):
+                x_codes[(g, e0 + i)] = codes[:, P * i:P * (i + 1)]
+                x_scales[(g, e0 + i)] = scales[:, P * i:P * (i + 1)]
+
+        def mx(acc, g, e, half, start, stop):
+            nc.tensor.matmul_mx(
+                out=acc[:],
+                lhsT=x_codes[(g, e)].bitcast(E5X4),
+                lhsT_scale=x_scales[(g, e)],
+                rhs=w_codes[half][:].bitcast(E5X4),
+                rhs_scale=w_scales[half][:],
+                start=start,
+                stop=stop,
+            )
+
+        def leave(acc, dst, scale, on_vector, name):
+            res = keep.tile([P, D], F32, name=name)
+            if on_vector:
+                if scale == 1.0:
+                    nc.vector.tensor_copy(out=res[:], in_=acc[:])
+                else:
+                    nc.vector.tensor_scalar(out=res[:], in0=acc[:], scalar1=scale, scalar2=None, op0=MULT)
+            else:
+                if scale == 1.0:
+                    nc.scalar.copy(out=res[:], in_=acc[:])
+                else:
+                    nc.scalar.activation(out=res[:], in_=acc[:], func=COPY, scale=scale)
+            nc.sync.dma_start(out=dst, in_=res[:])
+
+        def values(g, e, on_vector):
+            acc = psum.tile([P, D], F32, name="bank")
+            mx(acc, g, e, "v", True, True)
+            leave(acc, v_view[:, g, e, :], 1.0, on_vector, "v_res%d%d" % (g, e))
+
+        def landmarks(g, half, on_vector):
+            acc = psum.tile([P, D], F32, name="bank")
+            mx(acc, g, 0, half, True, False)
+            mx(acc, g, 1, half, False, True)
+            dst = vlm_view if half == "v" else klm_view
+            leave(acc, dst[:, g, :], 0.5, on_vector, "%slm_res%d" % (half, g))
+
+        load_w("v", 0)
+        load_w("v", 1)
+        for unit in units:
+            load_x(unit)
+        load_w("k", 0)
+        load_w("k", 1)
+
+        ident = keep.tile([P, P], F32, name="ident")
+        make_identity(nc, ident[:])
+        warm_in = keep.tile([P, 1], F32, name="warm_in")
+        warm_out = keep.tile([P, 1], F32, name="warm_out")
+        nc.vector.memset(warm_in[:], 0.0)
+        nc.scalar.activation(out=warm_out[:], in_=warm_in[:], func=COPY, scale=0.5)
+
+        interleave_w("v", 0)
+        interleave_w("v", 1)
+        transpose_x(units[0])
+        copy_x(units[0])
+        quantize_w("v", 0)
+        quantize_w("v", 1)
+        transpose_x(units[1])
+        copy_x(units[1])
+        quantize_x(units[0])
+        quantize_x(units[1])
+        transpose_x(units[2])
+        copy_x(units[2])
+        values(0, 0, True)
+        values(0, 1, False)
+        quantize_x(units[2])
+        transpose_x(units[3])
+        copy_x(units[3])
+        values(1, 0, True)
+        values(1, 1, False)
+        quantize_x(units[3])
+        interleave_w("k", 0)
+        transpose_x(units[4])
+        copy_x(units[4])
+        values(2, 0, True)
+        values(2, 1, False)
+        quantize_x(units[4])
+        interleave_w("k", 1)
+        landmarks(0, "v", True)
+        values(3, 0, False)
+        values(3, 1, True)
+        quantize_w("k", 0)
+        quantize_w("k", 1)
+        landmarks(1, "v", False)
+        landmarks(2, "v", True)
+        landmarks(3, "v", False)
+        landmarks(0, "k", True)
+        landmarks(1, "k", False)
+        landmarks(2, "k", True)
+        landmarks(3, "k", False)

@@ -19,16 +19,18 @@ PACK = 4
 GROUPS = 4
 W_PART = 256
 V_SHARE = 176
+SEPARATE_V = [0,1]
+WARM = 0
 
 
 def tile_ammattention_pa_kernel(tc, x, w_kv, out_0, out_1, out_2):
     nc = tc.nc
 
-    x_view = x.flatten_outer_dims().rearrange("(l m e) k -> m l e k", m=P, e=2)
+    x_view = x.flatten_outer_dims().rearrange("(m g e) k -> m g e k", g=GROUPS, e=2)
     w_view = w_kv.rearrange("(p j) n -> p j n", j=PACK)
-    v_view = out_0.flatten_outer_dims().rearrange("(l m e) d -> m l e d", m=P, e=2)
-    klm_view = out_1.flatten_outer_dims().rearrange("(l m) d -> m l d", m=P)
-    vlm_view = out_2.flatten_outer_dims().rearrange("(l m) d -> m l d", m=P)
+    v_view = out_0.flatten_outer_dims().rearrange("(m g e) d -> m g e d", g=GROUPS, e=2)
+    klm_view = out_1.flatten_outer_dims().rearrange("(m g) d -> m g d", g=GROUPS)
+    vlm_view = out_2.flatten_outer_dims().rearrange("(m g) d -> m g d", g=GROUPS)
 
     with ExitStack() as ctx:
         keep = ctx.enter_context(tc.tile_pool(name="keep", bufs=1))
@@ -36,7 +38,7 @@ def tile_ammattention_pa_kernel(tc, x, w_kv, out_0, out_1, out_2):
         ctx.enter_context(tc.manual_schedule())
 
         units = [(0, 0, 1), (0, 1, 1), (1, 0, 2), (2, 0, 2), (3, 0, 2)]
-        x_sb = {}
+        x_src = {}
         w_raw = {}
         w_grouped = {}
         w_codes = {}
@@ -45,44 +47,52 @@ def tile_ammattention_pa_kernel(tc, x, w_kv, out_0, out_1, out_2):
         x_grouped = {}
         x_codes = {}
         x_scales = {}
+        res_of = {}
 
-        def load_x(unit):
-            g, e0, n = unit
-            t = keep.tile([P, n, K], BF16, name="x_sb%d%d" % (g, e0))
-            nc.sync.dma_start(out=t[:], in_=x_view[:, g, e0:e0 + n, :])
-            x_sb[unit] = t
+        def load_x(g0, e0, rows):
+            t = keep.tile([P, rows, K], BF16, name="x_sb%d%d" % (g0, e0))
+            s0 = 2 * g0 + e0
+            nc.sync.dma_start(out=t[:], in_=x_view.rearrange("m g e k -> m (g e) k")[:, s0:s0 + rows, :])
+            for unit in units:
+                g, e, n = unit
+                s = 2 * g + e
+                if s0 <= s and s + n <= s0 + rows:
+                    x_src[unit] = t[:, s - s0:s - s0 + n, :]
 
-        def load_w(half, part):
-            c0 = (D if half == "v" else 0) + W_PART * part
-            t = keep.tile([P, PACK, W_PART], BF16, name="w_raw_%s%d" % (half, part))
-            nc.sync.dma_start(out=t[:], in_=w_view[:, :, c0:c0 + W_PART])
-            w_raw[(half, part)] = t
+        def load_w(half):
+            c0 = D if half == "v" else 0
+            t = keep.tile([P, PACK, D], BF16, name="w_raw_%s" % half)
+            nc.sync.dma_start(out=t[:], in_=w_view[:, :, c0:c0 + D])
+            w_raw[half] = t
+            grouped = keep.tile([P, D, PACK], BF16, name="w_grouped_%s" % half, align_bytes=64)
+            codes = keep.tile([P, D], U32, name="w_codes_%s" % half, align_bytes=64)
+            scales = keep.tile([P, D], U8, name="w_scales_%s" % half, align_bytes=64)
+            w_grouped[half] = grouped
+            w_codes[half] = codes
+            w_scales[half] = scales
 
         def interleave_w(half, part):
-            src = w_raw[(half, part)]
-            t = keep.tile([P, W_PART, PACK], BF16, name="w_grouped_%s%d" % (half, part), align_bytes=64)
-            nc.vector.tensor_copy(out=t[:, 0:V_SHARE, :], in_=src[:, :, 0:V_SHARE].rearrange("p j c -> p c j"))
-            nc.scalar.copy(out=t[:, V_SHARE:W_PART, :], in_=src[:, :, V_SHARE:W_PART].rearrange("p j c -> p c j"))
-            w_grouped[(half, part)] = t
+            src = w_raw[half]
+            dst = w_grouped[half]
+            a = W_PART * part
+            b = a + V_SHARE
+            c = a + W_PART
+            nc.vector.tensor_copy(out=dst[:, a:b, :], in_=src[:, :, a:b].rearrange("p j c -> p c j"))
+            nc.scalar.copy(out=dst[:, b:c, :], in_=src[:, :, b:c].rearrange("p j c -> p c j"))
 
         def quantize_w(half, part):
-            if part == 0:
-                codes = keep.tile([P, D], U32, name="w_codes_%s" % half, align_bytes=64)
-                scales = keep.tile([P, D], U8, name="w_scales_%s" % half, align_bytes=64)
-                w_codes[half] = codes
-                w_scales[half] = scales
             cols = slice(W_PART * part, W_PART * (part + 1))
             nc.vector.quantize_mx(
                 out=w_codes[half][:, cols].bitcast(E5X4),
                 scales=w_scales[half][:, cols],
-                in_=w_grouped[(half, part)][:].rearrange("p c j -> p (c j)"),
+                in_=w_grouped[half][:, cols, :].rearrange("p c j -> p (c j)"),
             )
 
         def transpose_x(unit):
             g, e0, n = unit
             xt = psum.tile([P, n, 2, P], F32, name="bank")
             for i in range(n):
-                words = x_sb[unit][:, i, :].bitcast(F32)
+                words = x_src[unit][:, i, :].bitcast(F32)
                 for u in range(2):
                     nc.tensor.transpose(xt[:, i, u, :], words[:, u:K // 2:2], ident[:])
             xt_of[unit] = xt
@@ -117,38 +127,53 @@ def tile_ammattention_pa_kernel(tc, x, w_kv, out_0, out_1, out_2):
                 stop=stop,
             )
 
-        def leave(acc, dst, scale, on_vector, name):
-            res = keep.tile([P, D], F32, name=name)
+        def leave(acc, res, scale, on_vector):
             if on_vector:
                 if scale == 1.0:
-                    nc.vector.tensor_copy(out=res[:], in_=acc[:])
+                    nc.vector.tensor_copy(out=res, in_=acc[:])
                 else:
-                    nc.vector.tensor_scalar(out=res[:], in0=acc[:], scalar1=scale, scalar2=None, op0=MULT)
+                    nc.vector.tensor_scalar(out=res, in0=acc[:], scalar1=scale, scalar2=None, op0=MULT)
             else:
                 if scale == 1.0:
-                    nc.scalar.copy(out=res[:], in_=acc[:])
+                    nc.scalar.copy(out=res, in_=acc[:])
                 else:
-                    nc.scalar.activation(out=res[:], in_=acc[:], func=COPY, scale=scale)
-            nc.sync.dma_start(out=dst, in_=res[:])
+                    nc.scalar.activation(out=res, in_=acc[:], func=COPY, scale=scale)
 
         def values(g, e, on_vector):
+            if e == 0:
+                t = keep.tile([P, 2, D], F32, name="v_res%d" % g)
+                res_of[("v", g)] = t
+            res = res_of[("v", g)]
             acc = psum.tile([P, D], F32, name="bank")
             mx(acc, g, e, "v", True, True)
-            leave(acc, v_view[:, g, e, :], 1.0, on_vector, "v_res%d%d" % (g, e))
+            leave(acc, res[:, e, :], 1.0, on_vector)
+            if g in SEPARATE_V:
+                nc.sync.dma_start(out=v_view[:, g, e, :], in_=res[:, e, :])
+            elif e == 1:
+                nc.sync.dma_start(out=v_view[:, g, :, :], in_=res[:])
 
         def landmarks(g, half, on_vector):
+            pair = g // 2
+            if g % 2 == 0:
+                t = keep.tile([P, 2, D], F32, name="%slm_res%d" % (half, pair))
+                res_of[(half + "lm", pair)] = t
+            res = res_of[(half + "lm", pair)]
             acc = psum.tile([P, D], F32, name="bank")
             mx(acc, g, 0, half, True, False)
             mx(acc, g, 1, half, False, True)
+            leave(acc, res[:, g % 2, :], 0.5, on_vector)
             dst = vlm_view if half == "v" else klm_view
-            leave(acc, dst[:, g, :], 0.5, on_vector, "%slm_res%d" % (half, g))
+            if half == "k" and pair == 1:
+                nc.sync.dma_start(out=dst[:, g, :], in_=res[:, g % 2, :])
+            elif g % 2 == 1:
+                nc.sync.dma_start(out=dst[:, 2 * pair:2 * pair + 2, :], in_=res[:])
 
-        load_w("v", 0)
-        load_w("v", 1)
-        for unit in units:
-            load_x(unit)
-        load_w("k", 0)
-        load_w("k", 1)
+        load_w("v")
+        load_x(0, 0, 1)
+        load_x(0, 1, 1)
+        load_x(1, 0, 2)
+        load_x(2, 0, 4)
+        load_w("k")
 
         ident = keep.tile([P, P], F32, name="ident")
         make_identity(nc, ident[:])

@@ -19,18 +19,16 @@ PACK = 4
 GROUPS = 4
 W_PART = 256
 V_SHARE = 176
-SEPARATE_V = [0,1]
-WARM = 0
 
 
 def tile_ammattention_pa_kernel(tc, x, w_kv, out_0, out_1, out_2):
     nc = tc.nc
 
-    x_view = x.flatten_outer_dims().rearrange("(m g e) k -> m g e k", g=GROUPS, e=2)
+    x_view = x.flatten_outer_dims().rearrange("(l m e) k -> m l e k", m=P, e=2)
     w_view = w_kv.rearrange("(p j) n -> p j n", j=PACK)
-    v_view = out_0.flatten_outer_dims().rearrange("(m g e) d -> m g e d", g=GROUPS, e=2)
-    klm_view = out_1.flatten_outer_dims().rearrange("(m g) d -> m g d", g=GROUPS)
-    vlm_view = out_2.flatten_outer_dims().rearrange("(m g) d -> m g d", g=GROUPS)
+    v_view = out_0.flatten_outer_dims().rearrange("(l m e) d -> m l e d", m=P, e=2)
+    klm_view = out_1.flatten_outer_dims().rearrange("(l m) d -> m l d", m=P)
+    vlm_view = out_2.flatten_outer_dims().rearrange("(l m) d -> m l d", m=P)
 
     with ExitStack() as ctx:
         keep = ctx.enter_context(tc.tile_pool(name="keep", bufs=1))
@@ -38,7 +36,7 @@ def tile_ammattention_pa_kernel(tc, x, w_kv, out_0, out_1, out_2):
         ctx.enter_context(tc.manual_schedule())
 
         units = [(0, 0, 1), (0, 1, 1), (1, 0, 2), (2, 0, 2), (3, 0, 2)]
-        x_src = {}
+        x_sb = {}
         w_raw = {}
         w_grouped = {}
         w_codes = {}
@@ -47,52 +45,44 @@ def tile_ammattention_pa_kernel(tc, x, w_kv, out_0, out_1, out_2):
         x_grouped = {}
         x_codes = {}
         x_scales = {}
-        res_of = {}
 
-        def load_x(g0, e0, rows):
-            t = keep.tile([P, rows, K], BF16, name="x_sb%d%d" % (g0, e0))
-            s0 = 2 * g0 + e0
-            nc.sync.dma_start(out=t[:], in_=x_view.rearrange("m g e k -> m (g e) k")[:, s0:s0 + rows, :])
-            for unit in units:
-                g, e, n = unit
-                s = 2 * g + e
-                if s0 <= s and s + n <= s0 + rows:
-                    x_src[unit] = t[:, s - s0:s - s0 + n, :]
+        def load_x(unit):
+            g, e0, n = unit
+            t = keep.tile([P, n, K], BF16, name="x_sb%d%d" % (g, e0))
+            nc.sync.dma_start(out=t[:], in_=x_view[:, g, e0:e0 + n, :])
+            x_sb[unit] = t
 
-        def load_w(half):
-            c0 = D if half == "v" else 0
-            t = keep.tile([P, PACK, D], BF16, name="w_raw_%s" % half)
-            nc.sync.dma_start(out=t[:], in_=w_view[:, :, c0:c0 + D])
-            w_raw[half] = t
-            grouped = keep.tile([P, D, PACK], BF16, name="w_grouped_%s" % half, align_bytes=64)
-            codes = keep.tile([P, D], U32, name="w_codes_%s" % half, align_bytes=64)
-            scales = keep.tile([P, D], U8, name="w_scales_%s" % half, align_bytes=64)
-            w_grouped[half] = grouped
-            w_codes[half] = codes
-            w_scales[half] = scales
+        def load_w(half, part):
+            c0 = (D if half == "v" else 0) + W_PART * part
+            t = keep.tile([P, PACK, W_PART], BF16, name="w_raw_%s%d" % (half, part))
+            nc.sync.dma_start(out=t[:], in_=w_view[:, :, c0:c0 + W_PART])
+            w_raw[(half, part)] = t
 
         def interleave_w(half, part):
-            src = w_raw[half]
-            dst = w_grouped[half]
-            a = W_PART * part
-            b = a + V_SHARE
-            c = a + W_PART
-            nc.vector.tensor_copy(out=dst[:, a:b, :], in_=src[:, :, a:b].rearrange("p j c -> p c j"))
-            nc.scalar.copy(out=dst[:, b:c, :], in_=src[:, :, b:c].rearrange("p j c -> p c j"))
+            src = w_raw[(half, part)]
+            t = keep.tile([P, W_PART, PACK], BF16, name="w_grouped_%s%d" % (half, part), align_bytes=64)
+            nc.vector.tensor_copy(out=t[:, 0:V_SHARE, :], in_=src[:, :, 0:V_SHARE].rearrange("p j c -> p c j"))
+            nc.scalar.copy(out=t[:, V_SHARE:W_PART, :], in_=src[:, :, V_SHARE:W_PART].rearrange("p j c -> p c j"))
+            w_grouped[(half, part)] = t
 
         def quantize_w(half, part):
+            if part == 0:
+                codes = keep.tile([P, D], U32, name="w_codes_%s" % half, align_bytes=64)
+                scales = keep.tile([P, D], U8, name="w_scales_%s" % half, align_bytes=64)
+                w_codes[half] = codes
+                w_scales[half] = scales
             cols = slice(W_PART * part, W_PART * (part + 1))
             nc.vector.quantize_mx(
                 out=w_codes[half][:, cols].bitcast(E5X4),
                 scales=w_scales[half][:, cols],
-                in_=w_grouped[half][:, cols, :].rearrange("p c j -> p (c j)"),
+                in_=w_grouped[(half, part)][:].rearrange("p c j -> p (c j)"),
             )
 
         def transpose_x(unit):
             g, e0, n = unit
             xt = psum.tile([P, n, 2, P], F32, name="bank")
             for i in range(n):
-                words = x_src[unit][:, i, :].bitcast(F32)
+                words = x_sb[unit][:, i, :].bitcast(F32)
                 for u in range(2):
                     nc.tensor.transpose(xt[:, i, u, :], words[:, u:K // 2:2], ident[:])
             xt_of[unit] = xt
@@ -127,53 +117,38 @@ def tile_ammattention_pa_kernel(tc, x, w_kv, out_0, out_1, out_2):
                 stop=stop,
             )
 
-        def leave(acc, res, scale, on_vector):
+        def leave(acc, dst, scale, on_vector, name):
+            res = keep.tile([P, D], F32, name=name)
             if on_vector:
                 if scale == 1.0:
-                    nc.vector.tensor_copy(out=res, in_=acc[:])
+                    nc.vector.tensor_copy(out=res[:], in_=acc[:])
                 else:
-                    nc.vector.tensor_scalar(out=res, in0=acc[:], scalar1=scale, scalar2=None, op0=MULT)
+                    nc.vector.tensor_scalar(out=res[:], in0=acc[:], scalar1=scale, scalar2=None, op0=MULT)
             else:
                 if scale == 1.0:
-                    nc.scalar.copy(out=res, in_=acc[:])
+                    nc.scalar.copy(out=res[:], in_=acc[:])
                 else:
-                    nc.scalar.activation(out=res, in_=acc[:], func=COPY, scale=scale)
+                    nc.scalar.activation(out=res[:], in_=acc[:], func=COPY, scale=scale)
+            nc.sync.dma_start(out=dst, in_=res[:])
 
         def values(g, e, on_vector):
-            if e == 0:
-                t = keep.tile([P, 2, D], F32, name="v_res%d" % g)
-                res_of[("v", g)] = t
-            res = res_of[("v", g)]
             acc = psum.tile([P, D], F32, name="bank")
             mx(acc, g, e, "v", True, True)
-            leave(acc, res[:, e, :], 1.0, on_vector)
-            if g in SEPARATE_V:
-                nc.sync.dma_start(out=v_view[:, g, e, :], in_=res[:, e, :])
-            elif e == 1:
-                nc.sync.dma_start(out=v_view[:, g, :, :], in_=res[:])
+            leave(acc, v_view[:, g, e, :], 1.0, on_vector, "v_res%d%d" % (g, e))
 
         def landmarks(g, half, on_vector):
-            pair = g // 2
-            if g % 2 == 0:
-                t = keep.tile([P, 2, D], F32, name="%slm_res%d" % (half, pair))
-                res_of[(half + "lm", pair)] = t
-            res = res_of[(half + "lm", pair)]
             acc = psum.tile([P, D], F32, name="bank")
             mx(acc, g, 0, half, True, False)
             mx(acc, g, 1, half, False, True)
-            leave(acc, res[:, g % 2, :], 0.5, on_vector)
             dst = vlm_view if half == "v" else klm_view
-            if half == "k" and pair == 1:
-                nc.sync.dma_start(out=dst[:, g, :], in_=res[:, g % 2, :])
-            elif g % 2 == 1:
-                nc.sync.dma_start(out=dst[:, 2 * pair:2 * pair + 2, :], in_=res[:])
+            leave(acc, dst[:, g, :], 0.5, on_vector, "%slm_res%d" % (half, g))
 
-        load_w("v")
-        load_x(0, 0, 1)
-        load_x(0, 1, 1)
-        load_x(1, 0, 2)
-        load_x(2, 0, 4)
-        load_w("k")
+        load_w("v", 0)
+        load_w("v", 1)
+        for unit in units:
+            load_x(unit)
+        load_w("k", 0)
+        load_w("k", 1)
 
         ident = keep.tile([P, P], F32, name="ident")
         make_identity(nc, ident[:])
@@ -182,13 +157,25 @@ def tile_ammattention_pa_kernel(tc, x, w_kv, out_0, out_1, out_2):
         nc.vector.memset(warm_in[:], 0.0)
         nc.scalar.activation(out=warm_out[:], in_=warm_in[:], func=COPY, scale=0.5)
 
+        dummy_sb = keep.tile([P, D], BF16, name="dummy_sb")
+        nc.vector.memset(dummy_sb[:], 0.0)
+
+        def dummy():
+            sink = psum.tile([P, D], F32, name="bank")
+            nc.tensor.matmul(sink[:], lhsT=dummy_sb[:, 0:P], rhs=dummy_sb[:], start=True, stop=True)
+
+        for i in range(4):
+            dummy()
+
         interleave_w("v", 0)
         interleave_w("v", 1)
         transpose_x(units[0])
+        dummy()
         copy_x(units[0])
         quantize_w("v", 0)
         quantize_w("v", 1)
         transpose_x(units[1])
+        dummy()
         copy_x(units[1])
         quantize_x(units[0])
         quantize_x(units[1])

@@ -13,10 +13,10 @@ U8 = mybir.dt.uint8
 E5X4 = mybir.dt.float8_e5m2_x4
 COPY = mybir.ActivationFunctionType.Copy
 MULT = mybir.AluOpType.mult
+ADD = mybir.AluOpType.add
 
 P = 128
 PACK = 4
-GROUPS = 4
 W_PART = 256
 V_SHARE = 176
 
@@ -35,7 +35,7 @@ def tile_ammattention_pa_kernel(tc, x, w_kv, out_0, out_1, out_2):
         psum = ctx.enter_context(tc.psum_pool(name="psum", bufs=8))
         ctx.enter_context(tc.manual_schedule())
 
-        units = [(0, 0, 1), (0, 1, 1), (1, 0, 2), (2, 0, 2), (3, 0, 2)]
+        X00, X01, X1, X2, X3 = (0, 0, 1), (0, 1, 1), (1, 0, 2), (2, 0, 2), (3, 0, 2)
         x_sb = {}
         w_raw = {}
         w_grouped = {}
@@ -65,8 +65,20 @@ def tile_ammattention_pa_kernel(tc, x, w_kv, out_0, out_1, out_2):
             nc.scalar.copy(out=t[:, V_SHARE:W_PART, :], in_=src[:, :, V_SHARE:W_PART].rearrange("p j c -> p c j"))
             w_grouped[(half, part)] = t
 
+        def interleave_w_pool(half, part, pieces):
+            src = w_raw[(half, part)]
+            t = keep.tile([P, W_PART, PACK], BF16, name="w_grouped_%s%d" % (half, part), align_bytes=64)
+            width = W_PART // pieces
+            for i in range(pieces):
+                cols = slice(width * i, width * (i + 1))
+                nc.gpsimd.tensor_scalar(
+                    out=t[:, cols, :], in0=src[:, :, cols].rearrange("p j c -> p c j"),
+                    scalar1=1.0, scalar2=0.0, op0=MULT, op1=ADD,
+                )
+            w_grouped[(half, part)] = t
+
         def quantize_w(half, part):
-            if part == 0:
+            if half not in w_codes:
                 codes = keep.tile([P, D], U32, name="w_codes_%s" % half, align_bytes=64)
                 scales = keep.tile([P, D], U8, name="w_scales_%s" % half, align_bytes=64)
                 w_codes[half] = codes
@@ -117,39 +129,53 @@ def tile_ammattention_pa_kernel(tc, x, w_kv, out_0, out_1, out_2):
                 stop=stop,
             )
 
-        def leave(acc, dst, scale, on_vector, name):
+        def leave(acc, dst, scale, on_vector, name, pieces=1):
             res = keep.tile([P, D], F32, name=name)
-            if on_vector:
-                if scale == 1.0:
-                    nc.vector.tensor_copy(out=res[:], in_=acc[:])
+            width = D // pieces
+            for i in range(pieces):
+                cols = slice(width * i, width * (i + 1))
+                if on_vector:
+                    if scale == 1.0:
+                        nc.vector.tensor_copy(out=res[:, cols], in_=acc[:, cols])
+                    else:
+                        nc.vector.tensor_scalar(out=res[:, cols], in0=acc[:, cols], scalar1=scale, scalar2=None, op0=MULT)
                 else:
-                    nc.vector.tensor_scalar(out=res[:], in0=acc[:], scalar1=scale, scalar2=None, op0=MULT)
-            else:
-                if scale == 1.0:
-                    nc.scalar.copy(out=res[:], in_=acc[:])
-                else:
-                    nc.scalar.activation(out=res[:], in_=acc[:], func=COPY, scale=scale)
-            nc.sync.dma_start(out=dst, in_=res[:])
+                    if scale == 1.0:
+                        nc.scalar.copy(out=res[:, cols], in_=acc[:, cols])
+                    else:
+                        nc.scalar.activation(out=res[:, cols], in_=acc[:, cols], func=COPY, scale=scale)
+                nc.sync.dma_start(out=dst[:, cols], in_=res[:, cols])
 
-        def values(g, e, on_vector):
+        def values(g, e, on_vector, pieces=1):
             acc = psum.tile([P, D], F32, name="bank")
             mx(acc, g, e, "v", True, True)
-            leave(acc, v_view[:, g, e, :], 1.0, on_vector, "v_res%d%d" % (g, e))
+            leave(acc, v_view[:, g, e, :], 1.0, on_vector, "v_res%d%d" % (g, e), pieces)
 
-        def landmarks(g, half, on_vector):
+        def landmarks(g, half, on_vector, pieces=1):
             acc = psum.tile([P, D], F32, name="bank")
             mx(acc, g, 0, half, True, False)
             mx(acc, g, 1, half, False, True)
             dst = vlm_view if half == "v" else klm_view
-            leave(acc, dst[:, g, :], 0.5, on_vector, "%slm_res%d" % (half, g))
+            leave(acc, dst[:, g, :], 0.5, on_vector, "%slm_res%d" % (half, g), pieces)
 
+        def dummy():
+            sink = psum.tile([P, D], F32, name="bank")
+            nc.tensor.matmul(sink[:], lhsT=dummy_sb[:, 0:P], rhs=dummy_sb[:], start=True, stop=True)
+
+        VEC, ACT = True, False
+
+        load_x(X00)
         load_w("v", 0)
+        load_x(X01)
         load_w("v", 1)
-        for unit in units:
-            load_x(unit)
+        load_x(X1)
         load_w("k", 0)
+        load_x(X2)
         load_w("k", 1)
+        load_x(X3)
 
+        dummy_sb = keep.tile([P, D], BF16, name="dummy_sb")
+        nc.vector.memset(dummy_sb[:], 0.0)
         ident = keep.tile([P, P], F32, name="ident")
         make_identity(nc, ident[:])
         warm_in = keep.tile([P, 1], F32, name="warm_in")
@@ -157,54 +183,47 @@ def tile_ammattention_pa_kernel(tc, x, w_kv, out_0, out_1, out_2):
         nc.vector.memset(warm_in[:], 0.0)
         nc.scalar.activation(out=warm_out[:], in_=warm_in[:], func=COPY, scale=0.5)
 
-        dummy_sb = keep.tile([P, D], BF16, name="dummy_sb")
-        nc.vector.memset(dummy_sb[:], 0.0)
-
-        def dummy():
-            sink = psum.tile([P, D], F32, name="bank")
-            nc.tensor.matmul(sink[:], lhsT=dummy_sb[:, 0:P], rhs=dummy_sb[:], start=True, stop=True)
-
-        for i in range(4):
-            dummy()
-
+        dummy()
+        dummy()
+        dummy()
+        transpose_x(X00)
+        dummy()
         interleave_w("v", 0)
-        interleave_w("v", 1)
-        transpose_x(units[0])
-        dummy()
-        copy_x(units[0])
+        transpose_x(X01)
         quantize_w("v", 0)
-        quantize_w("v", 1)
-        transpose_x(units[1])
+        copy_x(X00)
+        interleave_w("v", 1)
+        quantize_x(X00)
         dummy()
-        copy_x(units[1])
-        quantize_x(units[0])
-        quantize_x(units[1])
-        transpose_x(units[2])
-        copy_x(units[2])
-        values(0, 0, True)
-        values(0, 1, False)
-        quantize_x(units[2])
-        transpose_x(units[3])
-        copy_x(units[3])
-        values(1, 0, True)
-        values(1, 1, False)
-        quantize_x(units[3])
+        copy_x(X01)
+        transpose_x(X1)
+        quantize_w("v", 1)
+        copy_x(X1)
+        quantize_x(X01)
+        values(0, 0, VEC)
+        quantize_x(X1)
+        values(0, 1, ACT)
+        landmarks(0, "v", VEC)
         interleave_w("k", 0)
-        transpose_x(units[4])
-        copy_x(units[4])
-        values(2, 0, True)
-        values(2, 1, False)
-        quantize_x(units[4])
+        transpose_x(X2)
+        copy_x(X2)
+        quantize_x(X2)
+        values(1, 0, ACT)
+        values(1, 1, VEC)
         interleave_w("k", 1)
-        landmarks(0, "v", True)
-        values(3, 0, False)
-        values(3, 1, True)
+        landmarks(1, "v", ACT)
+        transpose_x(X3)
+        values(2, 0, ACT)
         quantize_w("k", 0)
+        copy_x(X3)
         quantize_w("k", 1)
-        landmarks(1, "v", False)
-        landmarks(2, "v", True)
-        landmarks(3, "v", False)
-        landmarks(0, "k", True)
-        landmarks(1, "k", False)
-        landmarks(2, "k", True)
-        landmarks(3, "k", False)
+        values(2, 1, VEC)
+        landmarks(2, "v", ACT)
+        quantize_x(X3)
+        landmarks(0, "k", VEC)
+        landmarks(1, "k", VEC)
+        values(3, 0, ACT)
+        values(3, 1, ACT)
+        landmarks(3, "v", VEC)
+        landmarks(2, "k", ACT)
+        landmarks(3, "k", VEC)

@@ -24,11 +24,18 @@ V_SHARE = 176
 def tile_ammattention_pa_kernel(tc, x, w_kv, out_0, out_1, out_2):
     nc = tc.nc
 
-    x_view = x.flatten_outer_dims().rearrange("(l m e) k -> m l e k", m=P, e=2)
+    x_view = x.flatten_outer_dims().rearrange("(m s) k -> m s k", s=8)
     w_view = w_kv.rearrange("(p j) n -> p j n", j=PACK)
-    v_view = out_0.flatten_outer_dims().rearrange("(l m e) d -> m l e d", m=P, e=2)
-    klm_view = out_1.flatten_outer_dims().rearrange("(l m) d -> m l d", m=P)
-    vlm_view = out_2.flatten_outer_dims().rearrange("(l m) d -> m l d", m=P)
+    out_views = {
+        "v": out_0.flatten_outer_dims().rearrange("(m s) d -> m s d", s=8),
+        "klm": out_1.flatten_outer_dims().rearrange("(m g) d -> m g d", g=4),
+        "vlm": out_2.flatten_outer_dims().rearrange("(m g) d -> m g d", g=4),
+    }
+    runs = {
+        "v": [[0], [1], [2], [3], [4, 5], [6, 7]],
+        "vlm": [[0], [1], [2], [3]],
+        "klm": [[0, 1], [2], [3]],
+    }
 
     with ExitStack() as ctx:
         keep = ctx.enter_context(tc.tile_pool(name="keep", bufs=1))
@@ -49,7 +56,7 @@ def tile_ammattention_pa_kernel(tc, x, w_kv, out_0, out_1, out_2):
         def load_x(unit):
             g, e0, n = unit
             t = keep.tile([P, n, K], BF16, name="x_sb%d%d" % (g, e0))
-            nc.sync.dma_start(out=t[:], in_=x_view[:, g, e0:e0 + n, :])
+            nc.sync.dma_start(out=t[:], in_=x_view[:, 2 * g + e0:2 * g + e0 + n, :])
             x_sb[unit] = t
 
         def load_w(half, part):
@@ -129,34 +136,38 @@ def tile_ammattention_pa_kernel(tc, x, w_kv, out_0, out_1, out_2):
                 stop=stop,
             )
 
-        def leave(acc, dst, scale, on_vector, name, pieces=1):
-            res = keep.tile([P, D], F32, name=name)
-            width = D // pieces
-            for i in range(pieces):
-                cols = slice(width * i, width * (i + 1))
-                if on_vector:
-                    if scale == 1.0:
-                        nc.vector.tensor_copy(out=res[:, cols], in_=acc[:, cols])
-                    else:
-                        nc.vector.tensor_scalar(out=res[:, cols], in0=acc[:, cols], scalar1=scale, scalar2=None, op0=MULT)
-                else:
-                    if scale == 1.0:
-                        nc.scalar.copy(out=res[:, cols], in_=acc[:, cols])
-                    else:
-                        nc.scalar.activation(out=res[:, cols], in_=acc[:, cols], func=COPY, scale=scale)
-                nc.sync.dma_start(out=dst[:, cols], in_=res[:, cols])
+        res_of = {}
 
-        def values(g, e, on_vector, pieces=1):
+        def leave(acc, kind, slot, scale, on_vector):
+            run = [r for r in runs[kind] if slot in r][0]
+            if slot == run[0]:
+                t = keep.tile([P, len(run), D], F32, name="%s_res%d" % (kind, slot))
+                res_of[(kind, run[0])] = t
+            res = res_of[(kind, run[0])]
+            dst = res[:, slot - run[0], :]
+            if on_vector:
+                if scale == 1.0:
+                    nc.vector.tensor_copy(out=dst, in_=acc[:])
+                else:
+                    nc.vector.tensor_scalar(out=dst, in0=acc[:], scalar1=scale, scalar2=None, op0=MULT)
+            else:
+                if scale == 1.0:
+                    nc.scalar.copy(out=dst, in_=acc[:])
+                else:
+                    nc.scalar.activation(out=dst, in_=acc[:], func=COPY, scale=scale)
+            if slot == run[-1]:
+                nc.sync.dma_start(out=out_views[kind][:, run[0]:run[-1] + 1, :], in_=res[:])
+
+        def values(g, e, on_vector):
             acc = psum.tile([P, D], F32, name="bank")
             mx(acc, g, e, "v", True, True)
-            leave(acc, v_view[:, g, e, :], 1.0, on_vector, "v_res%d%d" % (g, e), pieces)
+            leave(acc, "v", 2 * g + e, 1.0, on_vector)
 
-        def landmarks(g, half, on_vector, pieces=1):
+        def landmarks(g, half, on_vector):
             acc = psum.tile([P, D], F32, name="bank")
             mx(acc, g, 0, half, True, False)
             mx(acc, g, 1, half, False, True)
-            dst = vlm_view if half == "v" else klm_view
-            leave(acc, dst[:, g, :], 0.5, on_vector, "%slm_res%d" % (half, g), pieces)
+            leave(acc, half + "lm", g, 0.5, on_vector)
 
         def dummy():
             sink = psum.tile([P, D], F32, name="bank")
@@ -198,32 +209,32 @@ def tile_ammattention_pa_kernel(tc, x, w_kv, out_0, out_1, out_2):
         copy_x(X01)
         transpose_x(X1)
         quantize_w("v", 1)
-        copy_x(X1)
         quantize_x(X01)
-        values(0, 0, VEC)
-        quantize_x(X1)
-        values(0, 1, ACT)
-        landmarks(0, "v", VEC)
         interleave_w("k", 0)
+        copy_x(X1)
+        values(0, 0, VEC)
+        values(0, 1, ACT)
+        quantize_x(X1)
+        landmarks(0, "v", VEC)
         transpose_x(X2)
-        copy_x(X2)
-        quantize_x(X2)
-        values(1, 0, ACT)
-        values(1, 1, VEC)
         interleave_w("k", 1)
+        copy_x(X2)
+        values(1, 0, VEC)
+        values(1, 1, ACT)
+        quantize_x(X2)
+        quantize_w("k", 0)
+        quantize_w("k", 1)
         landmarks(1, "v", ACT)
         transpose_x(X3)
         values(2, 0, ACT)
-        quantize_w("k", 0)
         copy_x(X3)
-        quantize_w("k", 1)
         values(2, 1, VEC)
-        landmarks(2, "v", ACT)
         quantize_x(X3)
-        landmarks(0, "k", VEC)
+        landmarks(2, "v", ACT)
+        landmarks(0, "k", ACT)
         landmarks(1, "k", VEC)
         values(3, 0, ACT)
-        values(3, 1, ACT)
-        landmarks(3, "v", VEC)
-        landmarks(2, "k", ACT)
-        landmarks(3, "k", VEC)
+        values(3, 1, VEC)
+        landmarks(3, "v", ACT)
+        landmarks(2, "k", VEC)
+        landmarks(3, "k", ACT)

@@ -169,9 +169,10 @@ def tile_ammattention_pa_kernel(tc, x, w_kv, out_0, out_1, out_2):
             mx(acc, g, 1, half, False, True)
             leave(acc, half + "lm", g, 0.5, on_vector)
 
-        def dummy():
-            sink = psum.tile([P, D], F32, name="bank")
-            nc.tensor.matmul(sink[:], lhsT=dummy_sb[:, 0:P], rhs=dummy_sb[:], start=True, stop=True)
+        def dummy(n, moving=None):
+            rhs = dummy_sb[:] if moving is None else moving
+            for i in range(n):
+                nc.tensor.matmul(sink[:, 0:P], lhsT=dummy_sb[:], rhs=rhs, start=True, stop=True)
 
         VEC, ACT = True, False
 
@@ -185,8 +186,9 @@ def tile_ammattention_pa_kernel(tc, x, w_kv, out_0, out_1, out_2):
         load_w("k", 1)
         load_x(X3)
 
-        dummy_sb = keep.tile([P, D], BF16, name="dummy_sb")
+        dummy_sb = keep.tile([P, P], F32, name="dummy_sb")
         nc.vector.memset(dummy_sb[:], 0.0)
+        sink = psum.tile([P, D], F32, name="bank")
         ident = keep.tile([P, P], F32, name="ident")
         make_identity(nc, ident[:])
         warm_in = keep.tile([P, 1], F32, name="warm_in")
@@ -194,20 +196,19 @@ def tile_ammattention_pa_kernel(tc, x, w_kv, out_0, out_1, out_2):
         nc.vector.memset(warm_in[:], 0.0)
         nc.scalar.activation(out=warm_out[:], in_=warm_in[:], func=COPY, scale=0.5)
 
-        dummy()
-        dummy()
-        dummy()
+        dummy(3)
         transpose_x(X00)
-        dummy()
+        dummy(2)
         interleave_w("v", 0)
         transpose_x(X01)
         quantize_w("v", 0)
         copy_x(X00)
         interleave_w("v", 1)
         quantize_x(X00)
-        dummy()
+        dummy(2, w_raw[("v", 1)][:, 0, :].bitcast(F32))
         copy_x(X01)
         transpose_x(X1)
+        dummy(2, w_grouped[("v", 1)][:].rearrange("p c j -> p (c j)")[:, 0:2 * P].bitcast(F32))
         quantize_w("v", 1)
         quantize_x(X01)
         interleave_w("k", 0)

@@ -176,10 +176,10 @@ def tile_ammattention_pa_kernel(tc, x, w_kv, out_0, out_1, out_2):
 
         VEC, ACT = True, False
 
-        load_x(X00)
         load_w("v", 0)
-        load_x(X01)
+        load_x(X00)
         load_w("v", 1)
+        load_x(X01)
         load_x(X1)
         load_w("k", 0)
         load_x(X2)

@@ -208,7 +208,6 @@ def tile_ammattention_pa_kernel(tc, x, w_kv, out_0, out_1, out_2):
         dummy(2, w_raw[("v", 1)][:, 0, :].bitcast(F32))
         copy_x(X01)
         transpose_x(X1)
-        dummy(2, w_grouped[("v", 1)][:].rearrange("p c j -> p (c j)")[:, 0:2 * P].bitcast(F32))
         quantize_w("v", 1)
         quantize_x(X01)
         interleave_w("k", 0)

@@ -158,10 +158,28 @@ def tile_ammattention_pa_kernel(tc, x, w_kv, out_0, out_1, out_2):
             if slot == run[-1]:
                 nc.sync.dma_start(out=out_views[kind][:, run[0]:run[-1] + 1, :], in_=res[:])
 
+        acc_of = {}
+        sum_of = {}
+
         def values(g, e, on_vector):
             acc = psum.tile([P, D], F32, name="bank")
             mx(acc, g, e, "v", True, True)
             leave(acc, "v", 2 * g + e, 1.0, on_vector)
+            acc_of[(g, e)] = acc
+
+        def v_in_sbuf(slot):
+            run = [r for r in runs["v"] if slot in r][0]
+            return res_of[("v", run[0])][:, slot - run[0], :]
+
+        def mean_add(g, e_psum):
+            total = keep.tile([P, D], F32, name="v_sum%d" % g)
+            nc.vector.tensor_tensor(out=total[:], in0=acc_of[(g, e_psum)][:], in1=v_in_sbuf(2 * g + 1 - e_psum), op=ADD)
+            sum_of[g] = total
+
+        def mean_scale(g):
+            res = keep.tile([P, 1, D], F32, name="vlm_res%d" % g)
+            nc.vector.tensor_scalar(out=res[:, 0, :], in0=sum_of[g][:], scalar1=0.5, scalar2=None, op0=MULT)
+            nc.sync.dma_start(out=out_views["vlm"][:, g:g + 1, :], in_=res[:])
 
         def landmarks(g, half, on_vector):
             acc = psum.tile([P, D], F32, name="bank")
@@ -226,13 +244,14 @@ def tile_ammattention_pa_kernel(tc, x, w_kv, out_0, out_1, out_2):
         quantize_w("k", 1)
         landmarks(1, "v", ACT)
         transpose_x(X3)
-        values(2, 0, ACT)
         copy_x(X3)
-        values(2, 1, VEC)
+        values(2, 0, VEC)
+        values(2, 1, ACT)
         quantize_x(X3)
-        landmarks(2, "v", ACT)
+        mean_add(2, 0)
         landmarks(0, "k", ACT)
-        landmarks(1, "k", VEC)
+        landmarks(1, "k", ACT)
+        mean_scale(2)
         values(3, 0, ACT)
         values(3, 1, VEC)
         landmarks(3, "v", ACT)

@@ -34,7 +34,7 @@ def tile_ammattention_pa_kernel(tc, x, w_kv, out_0, out_1, out_2):
     runs = {
         "v": [[0], [1], [2], [3], [4, 5], [6, 7]],
         "vlm": [[0], [1], [2], [3]],
-        "klm": [[0, 1], [2], [3]],
+        "klm": [[0, 1], [2, 3]],
     }
 
     with ExitStack() as ctx:

@@ -32,8 +32,8 @@ def tile_ammattention_pa_kernel(tc, x, w_kv, out_0, out_1, out_2):
         "vlm": out_2.flatten_outer_dims().rearrange("(m g) d -> m g d", g=4),
     }
     runs = {
-        "v": [[0], [1], [2], [3], [4, 5], [6, 7]],
-        "vlm": [[0], [1], [2], [3]],
+        "v": [[0], [1], [2, 3], [4, 5], [6, 7]],
+        "vlm": [[0], [1], [2, 3]],
         "klm": [[0, 1], [2, 3]],
     }
 
@@ -177,9 +177,14 @@ def tile_ammattention_pa_kernel(tc, x, w_kv, out_0, out_1, out_2):
             sum_of[g] = total
 
         def mean_scale(g):
-            res = keep.tile([P, 1, D], F32, name="vlm_res%d" % g)
-            nc.vector.tensor_scalar(out=res[:, 0, :], in0=sum_of[g][:], scalar1=0.5, scalar2=None, op0=MULT)
-            nc.sync.dma_start(out=out_views["vlm"][:, g:g + 1, :], in_=res[:])
+            run = [r for r in runs["vlm"] if g in r][0]
+            if g == run[0]:
+                t = keep.tile([P, len(run), D], F32, name="vlm_res%d" % g)
+                res_of[("vlm", g)] = t
+            res = res_of[("vlm", run[0])]
+            nc.vector.tensor_scalar(out=res[:, g - run[0], :], in0=sum_of[g][:], scalar1=0.5, scalar2=None, op0=MULT)
+            if g == run[-1]:
+                nc.sync.dma_start(out=out_views["vlm"][:, run[0]:run[-1] + 1, :], in_=res[:])
 
         def landmarks(g, half, on_vector):
             acc = psum.tile([P, D], F32, name="bank")

@@ -19,6 +19,7 @@ P = 128
 PACK = 4
 W_PART = 256
 V_SHARE = 176
+V_ROWS_SHARE = 352
 
 
 def tile_ammattention_pa_kernel(tc, x, w_kv, out_0, out_1, out_2):
@@ -71,6 +72,35 @@ def tile_ammattention_pa_kernel(tc, x, w_kv, out_0, out_1, out_2):
             nc.vector.tensor_copy(out=t[:, 0:V_SHARE, :], in_=src[:, :, 0:V_SHARE].rearrange("p j c -> p c j"))
             nc.scalar.copy(out=t[:, V_SHARE:W_PART, :], in_=src[:, :, V_SHARE:W_PART].rearrange("p j c -> p c j"))
             w_grouped[(half, part)] = t
+
+        def load_w_rows(half, pair):
+            c0 = D if half == "v" else 0
+            t = keep.tile([P, 2, D], BF16, name="w_rows_%s%d" % (half, pair))
+            nc.sync.dma_start(out=t[:], in_=w_view[:, 2 * pair:2 * pair + 2, c0:c0 + D])
+            w_raw[(half, pair)] = t
+
+        def interleave_w_rows(half, pair):
+            src = w_raw[(half, pair)]
+            if half not in w_grouped:
+                t = keep.tile([P, D, PACK], BF16, name="w_grouped_%s" % half, align_bytes=64)
+                w_grouped[half] = t
+            t = w_grouped[half]
+            js = slice(2 * pair, 2 * pair + 2)
+            nc.vector.tensor_copy(out=t[:, 0:V_ROWS_SHARE, js], in_=src[:, :, 0:V_ROWS_SHARE].rearrange("p j c -> p c j"))
+            nc.scalar.copy(out=t[:, V_ROWS_SHARE:D, js], in_=src[:, :, V_ROWS_SHARE:D].rearrange("p j c -> p c j"))
+
+        def quantize_w_rows(half, part):
+            if half not in w_codes:
+                codes = keep.tile([P, D], U32, name="w_codes_%s" % half, align_bytes=64)
+                scales = keep.tile([P, D], U8, name="w_scales_%s" % half, align_bytes=64)
+                w_codes[half] = codes
+                w_scales[half] = scales
+            cols = slice(W_PART * part, W_PART * (part + 1))
+            nc.vector.quantize_mx(
+                out=w_codes[half][:, cols].bitcast(E5X4),
+                scales=w_scales[half][:, cols],
+                in_=w_grouped[half][:, cols, :].rearrange("p c j -> p (c j)"),
+            )
 
         def interleave_w_pool(half, part, pieces):
             src = w_raw[(half, part)]
@@ -199,14 +229,14 @@ def tile_ammattention_pa_kernel(tc, x, w_kv, out_0, out_1, out_2):
 
         VEC, ACT = True, False
 
-        load_w("v", 0)
+        load_w_rows("v", 0)
         load_x(X00)
-        load_w("v", 1)
+        load_w_rows("v", 1)
         load_x(X01)
         load_x(X1)
-        load_w("k", 0)
+        load_w_rows("k", 0)
         load_x(X2)
-        load_w("k", 1)
+        load_w_rows("k", 1)
         load_x(X3)
 
         dummy_sb = keep.tile([P, P], F32, name="dummy_sb")
@@ -222,31 +252,31 @@ def tile_ammattention_pa_kernel(tc, x, w_kv, out_0, out_1, out_2):
         dummy(3)
         transpose_x(X00)
         dummy(2)
-        interleave_w("v", 0)
+        interleave_w_rows("v", 0)
         transpose_x(X01)
-        quantize_w("v", 0)
         copy_x(X00)
-        interleave_w("v", 1)
+        interleave_w_rows("v", 1)
         quantize_x(X00)
-        dummy(2, w_raw[("v", 1)][:, 0, :].bitcast(F32))
+        dummy(2, w_raw[("v", 1)][:, 0, 0:W_PART].bitcast(F32))
         copy_x(X01)
         transpose_x(X1)
-        quantize_w("v", 1)
+        quantize_w_rows("v", 0)
+        quantize_w_rows("v", 1)
         quantize_x(X01)
-        interleave_w("k", 0)
+        interleave_w_rows("k", 0)
         copy_x(X1)
         values(0, 0, VEC)
         values(0, 1, ACT)
         quantize_x(X1)
         landmarks(0, "v", VEC)
         transpose_x(X2)
-        interleave_w("k", 1)
+        interleave_w_rows("k", 1)
         copy_x(X2)
         values(1, 0, VEC)
         values(1, 1, ACT)
         quantize_x(X2)
-        quantize_w("k", 0)
-        quantize_w("k", 1)
+        quantize_w_rows("k", 0)
+        quantize_w_rows("k", 1)
         landmarks(1, "v", ACT)
         transpose_x(X3)
         copy_x(X3)

@@ -197,6 +197,17 @@ def tile_ammattention_pa_kernel(tc, x, w_kv, out_0, out_1, out_2):
             leave(acc, "v", 2 * g + e, 1.0, on_vector)
             acc_of[(g, e)] = acc
 
+        def first_values():
+            acc = psum.tile([P, D], F32, name="bank")
+            mx(acc, 0, 0, "v", True, True)
+            res = keep.tile([P, 1, D], F32, name="v_res0")
+            res_of[("v", 0)] = res
+            for h in range(2):
+                cols = slice(h * D // 2, (h + 1) * D // 2)
+                nc.vector.tensor_copy(out=res[:, 0, cols], in_=acc[:, cols])
+                nc.sync.dma_start(out=out_views["v"][:, 0:1, cols], in_=res[:, :, cols])
+            acc_of[(0, 0)] = acc
+
         def v_in_sbuf(slot):
             run = [r for r in runs["v"] if slot in r][0]
             return res_of[("v", run[0])][:, slot - run[0], :]
@@ -265,7 +276,7 @@ def tile_ammattention_pa_kernel(tc, x, w_kv, out_0, out_1, out_2):
         quantize_x(X01)
         interleave_w_rows("k", 0)
         copy_x(X1)
-        values(0, 0, VEC)
+        first_values()
         values(0, 1, ACT)
         quantize_x(X1)
         landmarks(0, "v", VEC)

from contextlib import ExitStack

import concourse.mybir as mybir
from concourse.masks import make_identity

TOKENS, K, D = 1024, 512, 512
FLOPS = 2 * TOKENS * K * (2 * D)

F32 = mybir.dt.float32
BF16 = mybir.dt.bfloat16
U32 = mybir.dt.uint32
U8 = mybir.dt.uint8
E5X4 = mybir.dt.float8_e5m2_x4
COPY = mybir.ActivationFunctionType.Copy
MULT = mybir.AluOpType.mult
ADD = mybir.AluOpType.add

P = 128
PACK = 4
W_PART = 256
V_SHARE = 176
V_ROWS_SHARE = 352


def tile_ammattention_pa_kernel(tc, x, w_kv, out_0, out_1, out_2):
    nc = tc.nc

    x_view = x.flatten_outer_dims().rearrange("(m s) k -> m s k", s=8)
    w_view = w_kv.rearrange("(p j) n -> p j n", j=PACK)
    out_views = {
        "v": out_0.flatten_outer_dims().rearrange("(m s) d -> m s d", s=8),
        "klm": out_1.flatten_outer_dims().rearrange("(m g) d -> m g d", g=4),
        "vlm": out_2.flatten_outer_dims().rearrange("(m g) d -> m g d", g=4),
    }
    runs = {
        "v": [[0], [1], [2, 3], [4, 5], [6, 7]],
        "vlm": [[0], [1], [2, 3]],
        "klm": [[0, 1], [2, 3]],
    }

    with ExitStack() as ctx:
        keep = ctx.enter_context(tc.tile_pool(name="keep", bufs=1))
        psum = ctx.enter_context(tc.psum_pool(name="psum", bufs=8))
        ctx.enter_context(tc.manual_schedule())

        X00, X01, X1, X2, X3 = (0, 0, 1), (0, 1, 1), (1, 0, 2), (2, 0, 2), (3, 0, 2)
        x_sb = {}
        w_raw = {}
        w_grouped = {}
        w_codes = {}
        w_scales = {}
        xt_of = {}
        x_grouped = {}
        x_codes = {}
        x_scales = {}

        def load_x(unit):
            g, e0, n = unit
            t = keep.tile([P, n, K], BF16, name="x_sb%d%d" % (g, e0))
            nc.sync.dma_start(out=t[:], in_=x_view[:, 2 * g + e0:2 * g + e0 + n, :])
            x_sb[unit] = t

        def load_w(half, part):
            c0 = (D if half == "v" else 0) + W_PART * part
            t = keep.tile([P, PACK, W_PART], BF16, name="w_raw_%s%d" % (half, part))
            nc.sync.dma_start(out=t[:], in_=w_view[:, :, c0:c0 + W_PART])
            w_raw[(half, part)] = t

        def interleave_w(half, part):
            src = w_raw[(half, part)]
            t = keep.tile([P, W_PART, PACK], BF16, name="w_grouped_%s%d" % (half, part), align_bytes=64)
            nc.vector.tensor_copy(out=t[:, 0:V_SHARE, :], in_=src[:, :, 0:V_SHARE].rearrange("p j c -> p c j"))
            nc.scalar.copy(out=t[:, V_SHARE:W_PART, :], in_=src[:, :, V_SHARE:W_PART].rearrange("p j c -> p c j"))
            w_grouped[(half, part)] = t

        def load_w_rows(half, pair):
            c0 = D if half == "v" else 0
            t = keep.tile([P, 2, D], BF16, name="w_rows_%s%d" % (half, pair))
            nc.sync.dma_start(out=t[:], in_=w_view[:, 2 * pair:2 * pair + 2, c0:c0 + D])
            w_raw[(half, pair)] = t

        def interleave_w_rows(half, pair):
            src = w_raw[(half, pair)]
            if half not in w_grouped:
                t = keep.tile([P, D, PACK], BF16, name="w_grouped_%s" % half, align_bytes=64)
                w_grouped[half] = t
            t = w_grouped[half]
            js = slice(2 * pair, 2 * pair + 2)
            nc.vector.tensor_copy(out=t[:, 0:V_ROWS_SHARE, js], in_=src[:, :, 0:V_ROWS_SHARE].rearrange("p j c -> p c j"))
            nc.scalar.copy(out=t[:, V_ROWS_SHARE:D, js], in_=src[:, :, V_ROWS_SHARE:D].rearrange("p j c -> p c j"))

        def quantize_w_rows(half, part):
            if half not in w_codes:
                codes = keep.tile([P, D], U32, name="w_codes_%s" % half, align_bytes=64)
                scales = keep.tile([P, D], U8, name="w_scales_%s" % half, align_bytes=64)
                w_codes[half] = codes
                w_scales[half] = scales
            cols = slice(W_PART * part, W_PART * (part + 1))
            nc.vector.quantize_mx(
                out=w_codes[half][:, cols].bitcast(E5X4),
                scales=w_scales[half][:, cols],
                in_=w_grouped[half][:, cols, :].rearrange("p c j -> p (c j)"),
            )

        def interleave_w_pool(half, part, pieces):
            src = w_raw[(half, part)]
            t = keep.tile([P, W_PART, PACK], BF16, name="w_grouped_%s%d" % (half, part), align_bytes=64)
            width = W_PART // pieces
            for i in range(pieces):
                cols = slice(width * i, width * (i + 1))
                nc.gpsimd.tensor_scalar(
                    out=t[:, cols, :], in0=src[:, :, cols].rearrange("p j c -> p c j"),
                    scalar1=1.0, scalar2=0.0, op0=MULT, op1=ADD,
                )
            w_grouped[(half, part)] = t

        def quantize_w(half, part):
            if half not in w_codes:
                codes = keep.tile([P, D], U32, name="w_codes_%s" % half, align_bytes=64)
                scales = keep.tile([P, D], U8, name="w_scales_%s" % half, align_bytes=64)
                w_codes[half] = codes
                w_scales[half] = scales
            cols = slice(W_PART * part, W_PART * (part + 1))
            nc.vector.quantize_mx(
                out=w_codes[half][:, cols].bitcast(E5X4),
                scales=w_scales[half][:, cols],
                in_=w_grouped[(half, part)][:].rearrange("p c j -> p (c j)"),
            )

        def transpose_x(unit):
            g, e0, n = unit
            xt = psum.tile([P, n, 2, P], F32, name="bank")
            for i in range(n):
                words = x_sb[unit][:, i, :].bitcast(F32)
                for u in range(2):
                    nc.tensor.transpose(xt[:, i, u, :], words[:, u:K // 2:2], ident[:])
            xt_of[unit] = xt

        def copy_x(unit):
            g, e0, n = unit
            t = keep.tile([P, n, P, PACK], BF16, name="x_grouped%d%d" % (g, e0), align_bytes=64)
            nc.scalar.copy(out=t[:].bitcast(F32), in_=xt_of[unit][:].rearrange("p e u m -> p e m u"))
            x_grouped[unit] = t

        def quantize_x(unit):
            g, e0, n = unit
            codes = keep.tile([P, n * P], U32, name="x_codes%d%d" % (g, e0), align_bytes=64)
            scales = keep.tile([P, n * P], U8, name="x_scales%d%d" % (g, e0), align_bytes=64)
            nc.vector.quantize_mx(
                out=codes[:].bitcast(E5X4),
                scales=scales[:],
                in_=x_grouped[unit][:].rearrange("p e m t -> p (e m t)"),
            )
            for i in range(n):
                x_codes[(g, e0 + i)] = codes[:, P * i:P * (i + 1)]
                x_scales[(g, e0 + i)] = scales[:, P * i:P * (i + 1)]

        def mx(acc, g, e, half, start, stop):
            nc.tensor.matmul_mx(
                out=acc[:],
                lhsT=x_codes[(g, e)].bitcast(E5X4),
                lhsT_scale=x_scales[(g, e)],
                rhs=w_codes[half][:].bitcast(E5X4),
                rhs_scale=w_scales[half][:],
                start=start,
                stop=stop,
            )

        res_of = {}

        def leave(acc, kind, slot, scale, on_vector):
            run = [r for r in runs[kind] if slot in r][0]
            if slot == run[0]:
                t = keep.tile([P, len(run), D], F32, name="%s_res%d" % (kind, slot))
                res_of[(kind, run[0])] = t
            res = res_of[(kind, run[0])]
            dst = res[:, slot - run[0], :]
            if on_vector:
                if scale == 1.0:
                    nc.vector.tensor_copy(out=dst, in_=acc[:])
                else:
                    nc.vector.tensor_scalar(out=dst, in0=acc[:], scalar1=scale, scalar2=None, op0=MULT)
            else:
                if scale == 1.0:
                    nc.scalar.copy(out=dst, in_=acc[:])
                else:
                    nc.scalar.activation(out=dst, in_=acc[:], func=COPY, scale=scale)
            if slot == run[-1]:
                nc.sync.dma_start(out=out_views[kind][:, run[0]:run[-1] + 1, :], in_=res[:])

        acc_of = {}
        sum_of = {}

        def values(g, e, on_vector):
            acc = psum.tile([P, D], F32, name="bank")
            mx(acc, g, e, "v", True, True)
            leave(acc, "v", 2 * g + e, 1.0, on_vector)
            acc_of[(g, e)] = acc

        def first_values():
            acc = psum.tile([P, D], F32, name="bank")
            mx(acc, 0, 0, "v", True, True)
            res = keep.tile([P, 1, D], F32, name="v_res0")
            res_of[("v", 0)] = res
            for h in range(2):
                cols = slice(h * D // 2, (h + 1) * D // 2)
                nc.vector.tensor_copy(out=res[:, 0, cols], in_=acc[:, cols])
                nc.sync.dma_start(out=out_views["v"][:, 0:1, cols], in_=res[:, :, cols])
            acc_of[(0, 0)] = acc

        def v_in_sbuf(slot):
            run = [r for r in runs["v"] if slot in r][0]
            return res_of[("v", run[0])][:, slot - run[0], :]

        def mean_add(g, e_psum):
            total = keep.tile([P, D], F32, name="v_sum%d" % g)
            nc.vector.tensor_tensor(out=total[:], in0=acc_of[(g, e_psum)][:], in1=v_in_sbuf(2 * g + 1 - e_psum), op=ADD)
            sum_of[g] = total

        def mean_scale(g):
            run = [r for r in runs["vlm"] if g in r][0]
            if g == run[0]:
                t = keep.tile([P, len(run), D], F32, name="vlm_res%d" % g)
                res_of[("vlm", g)] = t
            res = res_of[("vlm", run[0])]
            nc.vector.tensor_scalar(out=res[:, g - run[0], :], in0=sum_of[g][:], scalar1=0.5, scalar2=None, op0=MULT)
            if g == run[-1]:
                nc.sync.dma_start(out=out_views["vlm"][:, run[0]:run[-1] + 1, :], in_=res[:])

        def landmarks(g, half, on_vector):
            acc = psum.tile([P, D], F32, name="bank")
            mx(acc, g, 0, half, True, False)
            mx(acc, g, 1, half, False, True)
            leave(acc, half + "lm", g, 0.5, on_vector)

        def dummy(n, moving=None):
            rhs = dummy_sb[:] if moving is None else moving
            for i in range(n):
                nc.tensor.matmul(sink[:, 0:P], lhsT=dummy_sb[:], rhs=rhs, start=True, stop=True)

        VEC, ACT = True, False

        load_w_rows("v", 0)
        load_x(X00)
        load_w_rows("v", 1)
        load_x(X01)
        load_x(X1)
        load_w_rows("k", 0)
        load_x(X2)
        load_w_rows("k", 1)
        load_x(X3)

        dummy_sb = keep.tile([P, P], F32, name="dummy_sb")
        nc.vector.memset(dummy_sb[:], 0.0)
        sink = psum.tile([P, D], F32, name="bank")
        ident = keep.tile([P, P], F32, name="ident")
        make_identity(nc, ident[:])
        warm_in = keep.tile([P, 1], F32, name="warm_in")
        warm_out = keep.tile([P, 1], F32, name="warm_out")
        nc.vector.memset(warm_in[:], 0.0)
        nc.scalar.activation(out=warm_out[:], in_=warm_in[:], func=COPY, scale=0.5)

        dummy(3)
        transpose_x(X00)
        dummy(2)
        interleave_w_rows("v", 0)
        transpose_x(X01)
        copy_x(X00)
        interleave_w_rows("v", 1)
        quantize_x(X00)
        dummy(2, w_raw[("v", 1)][:, 0, 0:W_PART].bitcast(F32))
        copy_x(X01)
        transpose_x(X1)
        quantize_w_rows("v", 0)
        quantize_w_rows("v", 1)
        quantize_x(X01)
        interleave_w_rows("k", 0)
        copy_x(X1)
        first_values()
        values(0, 1, ACT)
        quantize_x(X1)
        landmarks(0, "v", VEC)
        transpose_x(X2)
        interleave_w_rows("k", 1)
        copy_x(X2)
        values(1, 0, VEC)
        values(1, 1, ACT)
        quantize_x(X2)
        quantize_w_rows("k", 0)
        quantize_w_rows("k", 1)
        landmarks(1, "v", ACT)
        transpose_x(X3)
        copy_x(X3)
        values(2, 0, VEC)
        values(2, 1, ACT)
        quantize_x(X3)
        mean_add(2, 0)
        landmarks(0, "k", ACT)
        landmarks(1, "k", ACT)
        mean_scale(2)
        values(3, 0, ACT)
        values(3, 1, VEC)
        landmarks(3, "v", ACT)
        landmarks(2, "k", VEC)
        landmarks(3, "k", ACT)
